import numpy as np
import ml_dtypes


def mxq(x, axis, fmt="e4m3"):
    dtype, down = {"e4m3": (ml_dtypes.float8_e4m3fn, 7), "e5m2": (ml_dtypes.float8_e5m2, 14)}[fmt]
    v = np.moveaxis(np.asarray(x, np.float32).astype(ml_dtypes.bfloat16).astype(np.float64), axis, -1)
    blocks = v.reshape(v.shape[:-1] + (-1, 32))
    amax = np.abs(blocks).max(-1, keepdims=True)
    byte = np.maximum(np.where(amax > 0, np.frexp(amax)[1] - 1 + 127, 0) - down, 1)
    scale = np.exp2(byte - 127.0)
    codes = (blocks / scale).astype(np.float32).astype(dtype).astype(np.float64)
    return np.moveaxis((codes * scale).reshape(v.shape), -1, axis)


WIDE = False


def mx_kscale(k):
    if not WIDE:
        return np.ones(k)
    levels = np.array([18, -18])
    if k % 512:
        return np.exp2(np.random.permutation(np.resize(levels, k // 32))).repeat(32)
    a = np.empty((k // 512, 16))
    for p in range(k // 512):
        a[p, :8] = np.random.permutation(np.resize(levels, 8))
        for g in range(8):
            far = levels[np.abs(levels - a[p, g]) >= 10]
            a[p, g + 8] = far[np.random.randint(len(far))]
    return np.exp2(a.ravel()).repeat(32)


BF16 = ml_dtypes.bfloat16


def bf(x):
    return np.asarray(x, np.float32).astype(BF16)


def f64(x):
    return np.asarray(x).astype(np.float64)


B, N, HD, NH, KVH, D = 1, 1024, 1024, 8, 4, 128
QD = NH * D
KVD = KVH * D
EPS = 2.0 ** -23


def recip_rms(t):
    return 1.0 / np.sqrt(np.mean(t * t, axis=-1, keepdims=True) + EPS)


def join_heads(g, heads):
    return g.transpose(0, 2, 1, 3).reshape(B * N, heads * D)


def draw_grad(heads):
    return np.random.standard_normal((B, heads, N, D)) * np.exp2(np.random.randint(-6, 1, (B, 1, N, 1)))


def setup_inputs():
    s = mx_kscale(N)
    uq = mx_kscale(QD)
    uk = mx_kscale(KVD)
    uv = mx_kscale(KVD)
    rows = np.exp2(np.random.uniform(-2.0, 2.0, (B, N, 1)))
    tokens0 = bf(np.random.standard_normal((B, N, HD)) * rows)
    norm_w = bf(1.0 + 0.1 * np.random.standard_normal(HD))
    Wq0 = bf(np.random.standard_normal((QD, HD)) * 0.4 / np.sqrt(HD))
    bq = bf(np.random.standard_normal(QD) * 0.1)
    Wk0 = bf(np.random.standard_normal((KVD, HD)) * 0.4 / np.sqrt(HD))
    bk = bf(np.random.standard_normal(KVD) * 0.1)
    Wv0 = bf(np.random.standard_normal((KVD, HD)) / np.sqrt(HD))
    bv = bf(np.random.standard_normal(KVD) * 0.3)
    st = s[None, None, :, None]
    g0 = bf(draw_grad(NH) / st * uq.reshape(1, NH, 1, D))
    g1 = bf(draw_grad(KVH) / st * uk.reshape(1, KVH, 1, D))
    g2 = bf(draw_grad(KVH) / st * uv.reshape(1, KVH, 1, D))
    rstd = recip_rms(f64(tokens0))
    return {"tokens": bf(f64(tokens0) * s[None, :, None]),
            "norm_w": norm_w,
            "Wq": bf(f64(Wq0) / uq[:, None]),
            "bq": bq,
            "Wk": bf(f64(Wk0) / uk[:, None]),
            "bk": bk,
            "Wv": bf(f64(Wv0) / uv[:, None]),
            "bv": bv,
            "rstd": np.asarray(rstd, np.float32),
            "grad_0": g0,
            "grad_1": g1,
            "grad_2": g2}


def reference(tokens, norm_w, Wq, bq, Wk, bk, Wv, bv, rstd, grad_0, grad_1, grad_2):
    t = f64(tokens).reshape(B * N, HD)
    r = f64(rstd).reshape(B * N, 1)
    gain = f64(norm_w)
    x = t * r * gain
    dy = np.concatenate([join_heads(f64(grad_0), NH), join_heads(f64(grad_1), KVH), join_heads(f64(grad_2), KVH)], axis=1)
    w = np.concatenate([f64(Wq), f64(Wk), f64(Wv)], axis=0)
    dx = mxq(dy, 1, "e5m2") @ mxq(w, 0, "e4m3")
    dw = mxq(dy, 0, "e5m2").T @ mxq(x, 0, "e4m3")
    dh = dx * gain
    dt = r * (dh - t * r * r * np.mean(dh * t, axis=-1, keepdims=True))
    return dt.reshape(B, N, HD), dw[:QD], dw[QD:QD + KVD], dw[QD + KVD:]

@@ -1,0 +1,418 @@
+from contextlib import ExitStack
+
+import concourse.mybir as mybir
+from concourse.masks import make_identity
+
+F32 = mybir.dt.float32
+BF16 = mybir.dt.bfloat16
+U32 = mybir.dt.uint32
+U8 = mybir.dt.uint8
+E4M3X4 = mybir.dt.float8_e4m3fn_x4
+E5M2X4 = mybir.dt.float8_e5m2_x4
+MULT = mybir.AluOpType.mult
+ADD = mybir.AluOpType.add
+
+P = 128
+PACK = 4
+K_PASS = P * PACK
+HALF = 512
+N_TOK = 1024
+HD = 1024
+HEAD_DIM = 128
+GROUPS = N_TOK // K_PASS
+CHUNKS = 4
+HALVES = HD // HALF
+BANKS = 8
+FLOPS = 2 * 2 * N_TOK * HD * CHUNKS * K_PASS
+
+X_BUFS = 3
+PACK_BUFS = 6
+DWO_BUFS = 5
+DHR_BUFS = 4
+RES_BUFS = 2
+
+
+def tile_attentionlayerdecoder_pa_v_kernel(
+    tc, tokens, norm_w, Wq, bq, Wk, bk, Wv, bv, rstd, grad_0, grad_1, grad_2, out_0, out_1, out_2, out_3
+):
+    nc = tc.nc
+    grad_of = [(grad_0, 0), (grad_0, 4), (grad_1, 0), (grad_2, 0)]
+    w_of = [Wq[0:K_PASS, :], Wq[K_PASS : 2 * K_PASS, :], Wk, Wv]
+    dw_of = [out_1[0:K_PASS, :], out_1[K_PASS : 2 * K_PASS, :], out_2, out_3]
+
+    with ExitStack() as ctx:
+        keep = ctx.enter_context(tc.tile_pool(name="keep", bufs=1))
+        stage = ctx.enter_context(tc.tile_pool(name="stage", bufs=1))
+        psum = ctx.enter_context(tc.psum_pool(name="psum", bufs=1))
+        ctx.enter_context(tc.manual_schedule())
+
+        ident = keep.tile([P, P], F32, name="ident")
+        make_identity(nc, ident[:])
+        ident_bf = keep.tile([P, P], BF16, name="ident_bf")
+        gain = keep.tile([P, HD], F32, name="gain")
+        gain_cols_bf = keep.tile([P, HALVES, PACK], BF16, name="gain_cols_bf")
+        gain_cols = keep.tile([P, HALVES, PACK], F32, name="gain_cols")
+        r_col = keep.tile([P, GROUPS * PACK], F32, name="r_col")
+        r2_col = keep.tile([P, GROUPS * PACK], F32, name="r2_col")
+        coef = keep.tile([P, GROUPS * PACK], F32, name="coef")
+        t_sb = [keep.tile([P, PACK, HD], BF16, name="t%d" % g) for g in range(GROUPS)]
+        raw = {}
+        packed = {}
+        codes = {}
+        scales = {}
+        tiles = {}
+        free_banks = list(range(BANKS))
+        bank_of = {}
+
+        def new_bank(key, shape, dtype):
+            number = free_banks.pop(0)
+            bank = psum.tile(shape, dtype, name="bank", tag="bank%d" % number)
+            bank_of[key] = (number, bank)
+            return bank
+
+        def last_read(key):
+            number, bank = bank_of.pop(key)
+            free_banks.append(number)
+            return bank
+
+        def cols(h):
+            return slice(h * HALF, (h + 1) * HALF)
+
+        def copy_on(engine, out, in_):
+            if engine == "V":
+                nc.vector.tensor_copy(out=out, in_=in_)
+            else:
+                nc.scalar.copy(out=out, in_=in_)
+
+        def load_small():
+            nc.sync.dma_start(out=gain_cols_bf[:], in_=norm_w.rearrange("(h p i) -> p h i", h=HALVES, i=PACK))
+            nc.sync.dma_start(
+                out=r_col[:].rearrange("p (g j) -> p g j", g=GROUPS),
+                in_=rstd[0].rearrange("(g p j) o -> p g (j o)", g=GROUPS, j=PACK),
+            )
+
+        def load_t(g, h):
+            rows = tokens[0, g * K_PASS : (g + 1) * K_PASS, cols(h)]
+            nc.sync.dma_start(out=t_sb[g][:, :, cols(h)], in_=rows.rearrange("(p j) c -> p j c", j=PACK))
+
+        def load_w(c, h):
+            tile = keep.tile([P, PACK, HALF], BF16, name="w%d%d" % (c, h))
+            raw["W", c, h] = tile
+            nc.sync.dma_start(out=tile[:], in_=w_of[c][:, cols(h)].rearrange("(p j) n -> p j n", j=PACK))
+
+        def load_dy(g, c):
+            tile = keep.tile([P, PACK, K_PASS], BF16, name="dy%d%d" % (g, c))
+            raw["D", g, c] = tile
+            grad, first = grad_of[c]
+            for hh in range(K_PASS // HEAD_DIM):
+                rows = grad[0, first + hh, g * K_PASS : (g + 1) * K_PASS, :]
+                nc.sync.dma_start(
+                    out=tile[:, :, hh * HEAD_DIM : (hh + 1) * HEAD_DIM],
+                    in_=rows.rearrange("(p j) d -> p j d", j=PACK),
+                )
+
+        def consts_v():
+            nc.vector.tensor_copy(out=gain_cols[:], in_=gain_cols_bf[:])
+            nc.vector.scalar_tensor_tensor(
+                out=r2_col[:], in0=r_col[:], scalar=-1.0 / HD, in1=r_col[:], op0=MULT, op1=MULT
+            )
+
+        def ident_cast():
+            nc.vector.tensor_copy(out=ident_bf[:], in_=ident[:])
+
+        def gain_t(h):
+            bank = new_bank(("gain", h), [P, PACK, P], F32)
+            for i in range(PACK):
+                nc.tensor.transpose(bank[:, i, :], gain_cols[:, h, i : i + 1].to_broadcast([P, P]), ident[:])
+
+        def gain_c(h, engine):
+            copy_on(
+                engine,
+                gain[:, cols(h)].rearrange("p (n i) -> p n i", i=PACK),
+                last_read(("gain", h))[:].rearrange("p i n -> p n i"),
+            )
+
+        def xs(g, h, j):
+            if j == 0:
+                tile = stage.tile([P, PACK, HALF], BF16, name="x", tag="x", bufs=X_BUFS)
+                raw["X", g, h] = tile
+            col = g * PACK + j
+            nc.vector.scalar_tensor_tensor(
+                out=raw["X", g, h][:, j, :], in0=t_sb[g][:, j, cols(h)], scalar=r_col[:, col : col + 1],
+                in1=gain[:, cols(h)], op0=MULT, op1=MULT,
+            )
+
+        def new_packed(key):
+            tile = stage.tile([P, PACK * HALF], BF16, name="packed", tag="packed", bufs=PACK_BUFS, align_bytes=64)
+            packed[key] = tile
+            return tile
+
+        def il(kind, a, b, engine):
+            tile = new_packed((kind, a, b))
+            copy_on(
+                engine,
+                tile[:].rearrange("p (c i t) -> p c t i", i=4, t=PACK),
+                raw[kind, a, b][:].rearrange("p t (c i) -> p c t i", i=4),
+            )
+
+        def il_pe(kind, a, b):
+            for half in range(2):
+                bank = new_bank(("il", kind, a, b, half), [P, 2, HALF], BF16)
+                for q in range(2):
+                    first = (2 * half + q) * P
+                    nc.tensor.matmul(
+                        bank[:, q, :].rearrange("p (c t) -> p c t", t=PACK),
+                        lhsT=ident_bf[:],
+                        rhs=raw[kind, a, b][:, :, first : first + P].rearrange("p t c -> p c t"),
+                        start=True,
+                        stop=True,
+                    )
+
+        def il_c(kind, a, b, half, engine):
+            if half == 0:
+                new_packed((kind, a, b))
+            copy_on(
+                engine,
+                packed[kind, a, b][:, half * 2 * HALF : (half + 1) * 2 * HALF],
+                last_read(("il", kind, a, b, half))[:].rearrange("p q n -> p (q n)"),
+            )
+
+        def quant(kind, a, b):
+            name = "%s%d%d" % (kind, a, b)
+            code_tile = keep.tile([P, HALF], U32, name="codes" + name, align_bytes=64)
+            scale_tile = keep.tile([P, HALF], U8, name="scales" + name, align_bytes=64)
+            codes[kind, a, b] = code_tile
+            scales[kind, a, b] = scale_tile
+            fmt = E5M2X4 if kind in ("D", "T") else E4M3X4
+            nc.vector.quantize_mx(out=code_tile[:].bitcast(fmt), scales=scale_tile[:], in_=packed[kind, a, b][:])
+
+        def tr(g, c):
+            words = raw["D", g, c][:].rearrange("p j f -> p (j f)").bitcast(F32)
+            for b in range(2):
+                bank = new_bank(("T", g, c, b), [P, 2, 2, P], F32)
+                for jj in range(2):
+                    first = (2 * b + jj) * 2 * P
+                    for u in range(2):
+                        nc.tensor.transpose(bank[:, jj, u, :], words[:, first + u : first + 2 * P : 2], ident[:])
+
+        def tr_c(g, c, b, engine):
+            if b == 0:
+                new_packed(("T", g, c))
+            words = packed["T", g, c][:].bitcast(F32)
+            copy_on(
+                engine,
+                words[:, b * HALF : (b + 1) * HALF].rearrange("q (jj p u) -> q jj p u", jj=2, u=2),
+                last_read(("T", g, c, b))[:].rearrange("q jj u p -> q jj p u"),
+            )
+
+        def mx_group(bank, left, first, right):
+            for n in range(len(left)):
+                nc.tensor.matmul_mx(
+                    out=bank[:],
+                    lhsT=codes[left[n]][:, first : first + P].bitcast(E5M2X4),
+                    lhsT_scale=scales[left[n]][:, first : first + P],
+                    rhs=codes[right[n]][:].bitcast(E4M3X4),
+                    rhs_scale=scales[right[n]][:],
+                    start=(n == 0),
+                    stop=(n == len(left) - 1),
+                )
+
+        def dx(g, j, h):
+            bank = new_bank(("dx", g, j, h), [P, HALF], F32)
+            mx_group(bank, [("T", g, c) for c in range(CHUNKS)], j * P, [("W", c, h) for c in range(CHUNKS)])
+
+        def dw(c, m, h):
+            bank = new_bank(("dw", c, m, h), [P, HALF], F32)
+            mx_group(bank, [("D", g, c) for g in range(GROUPS)], m * P, [("X", g, h) for g in range(GROUPS)])
+
+        def dw_c(c, m, h, engine):
+            if ("dwo", c, m) not in tiles:
+                tile = stage.tile([P, HD], F32, name="dwo", tag="dwo", bufs=DWO_BUFS)
+                tiles["dwo", c, m] = tile
+            copy_on(engine, tiles["dwo", c, m][:, cols(h)], last_read(("dw", c, m, h))[:])
+
+        def dw_s(c, m):
+            nc.sync.dma_start(out=dw_of[c][m * P : (m + 1) * P, :], in_=tiles["dwo", c, m][:])
+
+        def dw_sh(c, m, h):
+            nc.sync.dma_start(out=dw_of[c][m * P : (m + 1) * P, cols(h)], in_=tiles["dwo", c, m][:, cols(h)])
+
+        def ep_a(g, j, h):
+            if h == 0:
+                tile = stage.tile([P, HD], F32, name="dhr", tag="dhr", bufs=DHR_BUFS)
+                tiles["dhr", g, j] = tile
+            col = g * PACK + j
+            nc.vector.scalar_tensor_tensor(
+                out=tiles["dhr", g, j][:, cols(h)], in0=last_read(("dx", g, j, h))[:], scalar=r_col[:, col : col + 1],
+                in1=gain[:, cols(h)], op0=MULT, op1=MULT,
+            )
+
+        def ep_b(g, j):
+            tile = stage.tile([P, HD], F32, name="res", tag="res", bufs=RES_BUFS)
+            tiles["res", g, j] = tile
+            col = g * PACK + j
+            nc.vector.scalar_tensor_tensor(
+                out=tile[:], in0=tiles["dhr", g, j][:], scalar=r2_col[:, col : col + 1], in1=t_sb[g][:, j, :],
+                op0=MULT, op1=MULT, accum_out=coef[:, col : col + 1],
+            )
+
+        def ep_c(g, j):
+            col = g * PACK + j
+            nc.vector.scalar_tensor_tensor(
+                out=tiles["res", g, j][:], in0=t_sb[g][:, j, :], scalar=coef[:, col : col + 1],
+                in1=tiles["dhr", g, j][:], op0=MULT, op1=ADD,
+            )
+
+        def ep_s(g, j):
+            rows = out_0[0, g * K_PASS : (g + 1) * K_PASS, :].rearrange("(p j) c -> p j c", j=PACK)
+            nc.sync.dma_start(out=rows[:, j, :], in_=tiles["res", g, j][:])
+
+        load_small()
+        load_dy(0, 0)
+        load_t(0, 0)
+        load_w(0, 0)
+        load_t(1, 0)
+        load_dy(1, 0)
+        load_t(0, 1)
+        load_w(1, 0)
+        load_t(1, 1)
+        load_dy(0, 1)
+        load_w(2, 0)
+        load_dy(0, 2)
+        load_w(3, 0)
+        load_dy(0, 3)
+        load_w(0, 1)
+        load_dy(1, 1)
+        load_w(1, 1)
+        load_w(2, 1)
+        load_w(3, 1)
+        load_dy(1, 2)
+        load_dy(1, 3)
+
+        def xs4(g, h):
+            for j in range(PACK):
+                xs(g, h, j)
+
+        def trc2(g, c):
+            tr_c(g, c, 0, "S")
+            tr_c(g, c, 1, "S")
+
+        consts_v()
+        gain_t(0)
+        gain_t(1)
+        gain_c(0, "S")
+        gain_c(1, "S")
+        il("D", 0, 0, "V")
+        tr(0, 0)
+        trc2(0, 0)
+        xs4(0, 0)
+        il("W", 0, 0, "S")
+        quant("D", 0, 0)
+        quant("T", 0, 0)
+        il("X", 0, 0, "S")
+        xs4(1, 0)
+        quant("W", 0, 0)
+        il("X", 1, 0, "S")
+        il("D", 1, 0, "V")
+        quant("X", 0, 0)
+        xs4(0, 1)
+        quant("D", 1, 0)
+        quant("X", 1, 0)
+        for m in range(4):
+            dw(0, m, 0)
+        tr(0, 1)
+        il("X", 0, 1, "S")
+        xs4(1, 1)
+        il("X", 1, 1, "S")
+        il("W", 1, 0, "V")
+        quant("X", 0, 1)
+        for m in range(4):
+            dw_c(0, m, 0, "S")
+        tr(0, 2)
+        tr(0, 3)
+        il("W", 2, 0, "V")
+        quant("W", 1, 0)
+        quant("X", 1, 1)
+        trc2(0, 1)
+        trc2(0, 2)
+        trc2(0, 3)
+        for m in range(4):
+            dw(0, m, 1)
+        il("W", 3, 0, "V")
+        quant("W", 2, 0)
+        quant("T", 0, 1)
+        il("W", 0, 1, "V")
+        quant("W", 3, 0)
+        quant("T", 0, 2)
+        for m in range(4):
+            dw_c(0, m, 1, "S")
+            dw_s(0, m)
+        quant("T", 0, 3)
+        for j in range(PACK):
+            dx(0, j, 0)
+        il("W", 1, 1, "V")
+        il("W", 2, 1, "S")
+        il("W", 3, 1, "S")
+        quant("W", 0, 1)
+        tr(1, 0)
+        tr(1, 1)
+        ep_a(0, 0, 0)
+        quant("W", 1, 1)
+        ep_a(0, 1, 0)
+        quant("W", 2, 1)
+        ep_a(0, 2, 0)
+        ep_a(0, 3, 0)
+        quant("W", 3, 1)
+        trc2(1, 0)
+        trc2(1, 1)
+        dx(0, 0, 1)
+        il("D", 0, 1, "S")
+        il("D", 1, 1, "S")
+        quant("T", 1, 0)
+        quant("T", 1, 1)
+        dx(0, 1, 1)
+        tr(1, 2)
+        tr(1, 3)
+        ep_a(0, 0, 1)
+        quant("D", 0, 1)
+        ep_b(0, 0)
+        ep_a(0, 1, 1)
+        ep_c(0, 0)
+        ep_s(0, 0)
+        trc2(1, 2)
+        trc2(1, 3)
+        dx(0, 2, 1)
+        dx(0, 3, 1)
+        quant("D", 1, 1)
+        ep_b(0, 1)
+        quant("T", 1, 2)
+        ep_c(0, 1)
+        ep_s(0, 1)
+        quant("T", 1, 3)
+        dsteps = [("D", g, c) for c in range(2, CHUNKS) for g in range(GROUPS)]
+        dwt = [(c, m) for c in range(1, CHUNKS) for m in range(4)]
+        for s in range(6):
+            g, j = divmod(s + 2, PACK)
+            if s < 4:
+                il(*dsteps[s], "S")
+            for c, m in dwt[2 * s : 2 * s + 2]:
+                dw(c, m, 0)
+                dw(c, m, 1)
+            if g == 1:
+                ep_a(g, j, 0)
+            if s > 0:
+                ep_c(*divmod(s + 1, PACK))
+                ep_s(*divmod(s + 1, PACK))
+            ep_a(g, j, 1)
+            if s < 4:
+                quant(*dsteps[s])
+            ep_b(g, j)
+            for c, m in dwt[2 * s : 2 * s + 2]:
+                dw_c(c, m, 0, "S")
+                dw_c(c, m, 1, "S")
+                dw_s(c, m)
+            if 1 <= s < 5:
+                dx(1, s - 1, 0)
+                dx(1, s - 1, 1)
+        ep_c(1, 3)
+        ep_s(1, 3)

@@ -11,6 +11,7 @@ E4M3X4 = mybir.dt.float8_e4m3fn_x4
 E5M2X4 = mybir.dt.float8_e5m2_x4
 MULT = mybir.AluOpType.mult
 ADD = mybir.AluOpType.add
+SUB = mybir.AluOpType.subtract
 
 P = 128
 PACK = 4
@@ -25,11 +26,7 @@ HALVES = HD // HALF
 BANKS = 8
 FLOPS = 2 * 2 * N_TOK * HD * CHUNKS * K_PASS
 
-X_BUFS = 3
-PACK_BUFS = 6
-DWO_BUFS = 5
-DHR_BUFS = 4
-RES_BUFS = 2
+SLOTS = 34
 
 
 def tile_attentionlayerdecoder_pa_v_kernel(
@@ -46,21 +43,22 @@ def tile_attentionlayerdecoder_pa_v_kernel(
         psum = ctx.enter_context(tc.psum_pool(name="psum", bufs=1))
         ctx.enter_context(tc.manual_schedule())
 
+        ident_bf = keep.tile([P, P], BF16, name="ident_bf")
+        make_identity(nc, ident_bf[:])
+        gain = keep.tile([P, HD], BF16, name="gain")
+        r_parts = keep.tile([P, GROUPS * PACK, P], BF16, name="r_parts")
+        r_rows = keep.tile([P, GROUPS * PACK, P], BF16, name="r_rows")
+        r_rest = keep.tile([P, GROUPS * PACK], F32, name="r_rest")
+        nc.gpsimd.memset(r_parts[:].rearrange("p a b -> p (a b)").bitcast(F32), 0.0)
         ident = keep.tile([P, P], F32, name="ident")
         make_identity(nc, ident[:])
-        ident_bf = keep.tile([P, P], BF16, name="ident_bf")
-        gain = keep.tile([P, HD], F32, name="gain")
         gain_cols_bf = keep.tile([P, HALVES, PACK], BF16, name="gain_cols_bf")
-        gain_cols = keep.tile([P, HALVES, PACK], F32, name="gain_cols")
         r_col = keep.tile([P, GROUPS * PACK], F32, name="r_col")
         r2_col = keep.tile([P, GROUPS * PACK], F32, name="r2_col")
         coef = keep.tile([P, GROUPS * PACK], F32, name="coef")
         t_sb = [keep.tile([P, PACK, HD], BF16, name="t%d" % g) for g in range(GROUPS)]
-        raw = {}
-        packed = {}
         codes = {}
         scales = {}
-        tiles = {}
         free_banks = list(range(BANKS))
         bank_of = {}
 
@@ -74,6 +72,22 @@ def tile_attentionlayerdecoder_pa_v_kernel(
             number, bank = bank_of.pop(key)
             free_banks.append(number)
             return bank
+
+        free_slots = list(range(SLOTS))
+        slot_of = {}
+
+        def new_slot(key, shape, dtype, uses):
+            number = free_slots.pop(0)
+            tile = stage.tile(shape, dtype, name="slot", tag="slot%d" % number, align_bytes=64)
+            slot_of[key] = [number, tile, uses]
+            return tile
+
+        def use(key):
+            entry = slot_of[key]
+            entry[2] = entry[2] - 1
+            if entry[2] == 0:
+                free_slots.append(entry[0])
+            return entry[1]
 
         def cols(h):
             return slice(h * HALF, (h + 1) * HALF)
@@ -96,13 +110,11 @@ def tile_attentionlayerdecoder_pa_v_kernel(
             nc.sync.dma_start(out=t_sb[g][:, :, cols(h)], in_=rows.rearrange("(p j) c -> p j c", j=PACK))
 
         def load_w(c, h):
-            tile = keep.tile([P, PACK, HALF], BF16, name="w%d%d" % (c, h))
-            raw["W", c, h] = tile
+            tile = new_slot(("raw", "W", c, h), [P, PACK, HALF], BF16, 1)
             nc.sync.dma_start(out=tile[:], in_=w_of[c][:, cols(h)].rearrange("(p j) n -> p j n", j=PACK))
 
         def load_dy(g, c):
-            tile = keep.tile([P, PACK, K_PASS], BF16, name="dy%d%d" % (g, c))
-            raw["D", g, c] = tile
+            tile = new_slot(("raw", "D", g, c), [P, PACK, K_PASS], BF16, 2)
             grad, first = grad_of[c]
             for hh in range(K_PASS // HEAD_DIM):
                 rows = grad[0, first + hh, g * K_PASS : (g + 1) * K_PASS, :]
@@ -112,18 +124,14 @@ def tile_attentionlayerdecoder_pa_v_kernel(
                 )
 
         def consts_v():
-            nc.vector.tensor_copy(out=gain_cols[:], in_=gain_cols_bf[:])
             nc.vector.scalar_tensor_tensor(
                 out=r2_col[:], in0=r_col[:], scalar=-1.0 / HD, in1=r_col[:], op0=MULT, op1=MULT
             )
 
-        def ident_cast():
-            nc.vector.tensor_copy(out=ident_bf[:], in_=ident[:])
-
         def gain_t(h):
-            bank = new_bank(("gain", h), [P, PACK, P], F32)
+            bank = new_bank(("gain", h), [P, PACK, P], BF16)
             for i in range(PACK):
-                nc.tensor.transpose(bank[:, i, :], gain_cols[:, h, i : i + 1].to_broadcast([P, P]), ident[:])
+                nc.tensor.transpose(bank[:, i, :], gain_cols_bf[:, h, i : i + 1].to_broadcast([P, P]), ident_bf[:])
 
         def gain_c(h, engine):
             copy_on(
@@ -132,30 +140,54 @@ def tile_attentionlayerdecoder_pa_v_kernel(
                 last_read(("gain", h))[:].rearrange("p i n -> p n i"),
             )
 
-        def xs(g, h, j):
-            if j == 0:
-                tile = stage.tile([P, PACK, HALF], BF16, name="x", tag="x", bufs=X_BUFS)
-                raw["X", g, h] = tile
-            col = g * PACK + j
-            nc.vector.scalar_tensor_tensor(
-                out=raw["X", g, h][:, j, :], in0=t_sb[g][:, j, cols(h)], scalar=r_col[:, col : col + 1],
-                in1=gain[:, cols(h)], op0=MULT, op1=MULT,
+        def r_split():
+            nc.vector.tensor_copy(out=r_parts[:, :, 0], in_=r_col[:])
+            nc.vector.tensor_tensor(out=r_rest[:], in0=r_col[:], in1=r_parts[:, :, 0], op=SUB)
+            nc.vector.tensor_copy(out=r_parts[:, :, 1], in_=r_rest[:])
+            nc.vector.tensor_tensor(out=r_parts[:, :, 2], in0=r_rest[:], in1=r_parts[:, :, 1], op=SUB)
+
+        def r_t():
+            bank = new_bank("r", [P, GROUPS * PACK, P], BF16)
+            for col in range(GROUPS * PACK):
+                nc.tensor.transpose(bank[:, col, :], r_parts[:, col, :], ident_bf[:])
+
+        def r_c():
+            nc.scalar.copy(out=r_rows[:], in_=last_read("r")[:])
+
+        def rg(g, h, q):
+            bank = new_bank(("rg", g, h, q), [P, PACK, P], F32)
+            first = h * HALF + q * P
+            for j in range(PACK):
+                nc.tensor.matmul(
+                    bank[:, j, :], lhsT=r_rows[:, g * PACK + j, :], rhs=gain[:, first : first + P], start=True, stop=True
+                )
+
+        def xs(g, h, q):
+            if q == 0:
+                new_packed(("X", g, h))
+            first = h * HALF + q * P
+            nc.vector.tensor_tensor(
+                out=slot_of["packed", "X", g, h][1][:, q * HALF : (q + 1) * HALF].rearrange(
+                    "p (c i j) -> p c j i", i=4, j=PACK
+                ),
+                in0=last_read(("rg", g, h, q))[:].rearrange("p j (c i) -> p c j i", i=4),
+                in1=t_sb[g][:, :, first : first + P].rearrange("p j (c i) -> p c j i", i=4),
+                op=MULT,
             )
 
         def new_packed(key):
-            tile = stage.tile([P, PACK * HALF], BF16, name="packed", tag="packed", bufs=PACK_BUFS, align_bytes=64)
-            packed[key] = tile
-            return tile
+            return new_slot(("packed",) + key, [P, PACK * HALF], BF16, 1)
 
         def il(kind, a, b, engine):
             tile = new_packed((kind, a, b))
             copy_on(
                 engine,
                 tile[:].rearrange("p (c i t) -> p c t i", i=4, t=PACK),
-                raw[kind, a, b][:].rearrange("p t (c i) -> p c t i", i=4),
+                use(("raw", kind, a, b))[:].rearrange("p t (c i) -> p c t i", i=4),
             )
 
         def il_pe(kind, a, b):
+            source = use(("raw", kind, a, b))
             for half in range(2):
                 bank = new_bank(("il", kind, a, b, half), [P, 2, HALF], BF16)
                 for q in range(2):
@@ -163,7 +195,7 @@ def tile_attentionlayerdecoder_pa_v_kernel(
                     nc.tensor.matmul(
                         bank[:, q, :].rearrange("p (c t) -> p c t", t=PACK),
                         lhsT=ident_bf[:],
-                        rhs=raw[kind, a, b][:, :, first : first + P].rearrange("p t c -> p c t"),
+                        rhs=source[:, :, first : first + P].rearrange("p t c -> p c t"),
                         start=True,
                         stop=True,
                     )
@@ -173,7 +205,7 @@ def tile_attentionlayerdecoder_pa_v_kernel(
                 new_packed((kind, a, b))
             copy_on(
                 engine,
-                packed[kind, a, b][:, half * 2 * HALF : (half + 1) * 2 * HALF],
+                slot_of["packed", kind, a, b][1][:, half * 2 * HALF : (half + 1) * 2 * HALF],
                 last_read(("il", kind, a, b, half))[:].rearrange("p q n -> p (q n)"),
             )
 
@@ -184,10 +216,10 @@ def tile_attentionlayerdecoder_pa_v_kernel(
             codes[kind, a, b] = code_tile
             scales[kind, a, b] = scale_tile
             fmt = E5M2X4 if kind in ("D", "T") else E4M3X4
-            nc.vector.quantize_mx(out=code_tile[:].bitcast(fmt), scales=scale_tile[:], in_=packed[kind, a, b][:])
+            nc.vector.quantize_mx(out=code_tile[:].bitcast(fmt), scales=scale_tile[:], in_=use(("packed", kind, a, b))[:])
 
         def tr(g, c):
-            words = raw["D", g, c][:].rearrange("p j f -> p (j f)").bitcast(F32)
+            words = use(("raw", "D", g, c))[:].rearrange("p j f -> p (j f)").bitcast(F32)
             for b in range(2):
                 bank = new_bank(("T", g, c, b), [P, 2, 2, P], F32)
                 for jj in range(2):
@@ -198,7 +230,7 @@ def tile_attentionlayerdecoder_pa_v_kernel(
         def tr_c(g, c, b, engine):
             if b == 0:
                 new_packed(("T", g, c))
-            words = packed["T", g, c][:].bitcast(F32)
+            words = slot_of["packed", "T", g, c][1][:].bitcast(F32)
             copy_on(
                 engine,
                 words[:, b * HALF : (b + 1) * HALF].rearrange("q (jj p u) -> q jj p u", jj=2, u=2),
@@ -226,193 +258,238 @@ def tile_attentionlayerdecoder_pa_v_kernel(
             mx_group(bank, [("D", g, c) for g in range(GROUPS)], m * P, [("X", g, h) for g in range(GROUPS)])
 
         def dw_c(c, m, h, engine):
-            if ("dwo", c, m) not in tiles:
-                tile = stage.tile([P, HD], F32, name="dwo", tag="dwo", bufs=DWO_BUFS)
-                tiles["dwo", c, m] = tile
-            copy_on(engine, tiles["dwo", c, m][:, cols(h)], last_read(("dw", c, m, h))[:])
+            if ("dwo", c, m) not in slot_of:
+                new_slot(("dwo", c, m), [P, HD], F32, 2)
+            copy_on(engine, slot_of["dwo", c, m][1][:, cols(h)], last_read(("dw", c, m, h))[:])
 
         def dw_s(c, m):
-            nc.sync.dma_start(out=dw_of[c][m * P : (m + 1) * P, :], in_=tiles["dwo", c, m][:])
+            use(("dwo", c, m))
+            nc.sync.dma_start(out=dw_of[c][m * P : (m + 1) * P, :], in_=use(("dwo", c, m))[:])
 
         def dw_sh(c, m, h):
-            nc.sync.dma_start(out=dw_of[c][m * P : (m + 1) * P, cols(h)], in_=tiles["dwo", c, m][:, cols(h)])
+            nc.sync.dma_start(out=dw_of[c][m * P : (m + 1) * P, cols(h)], in_=use(("dwo", c, m))[:, cols(h)])
 
         def ep_a(g, j, h):
             if h == 0:
-                tile = stage.tile([P, HD], F32, name="dhr", tag="dhr", bufs=DHR_BUFS)
-                tiles["dhr", g, j] = tile
+                new_slot(("dhr", g, j), [P, HD], F32, 2)
             col = g * PACK + j
             nc.vector.scalar_tensor_tensor(
-                out=tiles["dhr", g, j][:, cols(h)], in0=last_read(("dx", g, j, h))[:], scalar=r_col[:, col : col + 1],
+                out=slot_of["dhr", g, j][1][:, cols(h)], in0=last_read(("dx", g, j, h))[:], scalar=r_col[:, col : col + 1],
                 in1=gain[:, cols(h)], op0=MULT, op1=MULT,
             )
 
         def ep_b(g, j):
-            tile = stage.tile([P, HD], F32, name="res", tag="res", bufs=RES_BUFS)
-            tiles["res", g, j] = tile
+            tile = new_slot(("res", g, j), [P, HD], F32, 1)
             col = g * PACK + j
             nc.vector.scalar_tensor_tensor(
-                out=tile[:], in0=tiles["dhr", g, j][:], scalar=r2_col[:, col : col + 1], in1=t_sb[g][:, j, :],
+                out=tile[:], in0=use(("dhr", g, j))[:], scalar=r2_col[:, col : col + 1], in1=t_sb[g][:, j, :],
                 op0=MULT, op1=MULT, accum_out=coef[:, col : col + 1],
             )
 
         def ep_c(g, j):
             col = g * PACK + j
             nc.vector.scalar_tensor_tensor(
-                out=tiles["res", g, j][:], in0=t_sb[g][:, j, :], scalar=coef[:, col : col + 1],
-                in1=tiles["dhr", g, j][:], op0=MULT, op1=ADD,
+                out=slot_of["res", g, j][1][:], in0=t_sb[g][:, j, :], scalar=coef[:, col : col + 1],
+                in1=use(("dhr", g, j))[:], op0=MULT, op1=ADD,
             )
+
+        def ep_ch(g, j, h):
+            col = g * PACK + j
+            res = slot_of["res", g, j][1]
+            nc.vector.scalar_tensor_tensor(
+                out=res[:, cols(h)], in0=t_sb[g][:, j, cols(h)], scalar=coef[:, col : col + 1],
+                in1=slot_of["dhr", g, j][1][:, cols(h)], op0=MULT, op1=ADD,
+            )
+            rows = out_0[0, g * K_PASS : (g + 1) * K_PASS, cols(h)].rearrange("(p j) c -> p j c", j=PACK)
+            nc.sync.dma_start(out=rows[:, j, :], in_=res[:, cols(h)])
 
         def ep_s(g, j):
             rows = out_0[0, g * K_PASS : (g + 1) * K_PASS, :].rearrange("(p j) c -> p j c", j=PACK)
-            nc.sync.dma_start(out=rows[:, j, :], in_=tiles["res", g, j][:])
+            nc.sync.dma_start(out=rows[:, j, :], in_=use(("res", g, j))[:])
 
         load_small()
         load_dy(0, 0)
-        load_t(0, 0)
         load_w(0, 0)
-        load_t(1, 0)
+        load_t(0, 0)
         load_dy(1, 0)
-        load_t(0, 1)
+        load_t(1, 0)
         load_w(1, 0)
-        load_t(1, 1)
+        load_t(0, 1)
         load_dy(0, 1)
+        load_t(1, 1)
         load_w(2, 0)
         load_dy(0, 2)
         load_w(3, 0)
         load_dy(0, 3)
-        load_w(0, 1)
-        load_dy(1, 1)
-        load_w(1, 1)
-        load_w(2, 1)
-        load_w(3, 1)
-        load_dy(1, 2)
-        load_dy(1, 3)
+        for c in range(CHUNKS):
+            load_w(c, 1)
+        for c in range(1, CHUNKS):
+            load_dy(1, c)
+
+        def rg4(g, h):
+            for q in range(PACK):
+                rg(g, h, q)
 
         def xs4(g, h):
-            for j in range(PACK):
-                xs(g, h, j)
+            for q in range(PACK):
+                xs(g, h, q)
 
         def trc2(g, c):
             tr_c(g, c, 0, "S")
             tr_c(g, c, 1, "S")
 
-        consts_v()
+        def dw2(c, m):
+            dw(c, m, 0)
+            dw(c, m, 1)
+
+        def out2(c, m):
+            dw_c(c, m, 0, "S")
+            dw_c(c, m, 1, "S")
+            dw_s(c, m)
+
+
+        r_split()
         gain_t(0)
         gain_t(1)
+        r_t()
         gain_c(0, "S")
+        r_c()
         gain_c(1, "S")
         il("D", 0, 0, "V")
+        il("W", 0, 0, "V")
         tr(0, 0)
+        rg4(0, 0)
         trc2(0, 0)
-        xs4(0, 0)
-        il("W", 0, 0, "S")
+        rg4(1, 0)
+        il("D", 1, 0, "S")
+        il("W", 1, 0, "S")
+        il("D", 0, 1, "S")
         quant("D", 0, 0)
-        quant("T", 0, 0)
-        il("X", 0, 0, "S")
-        xs4(1, 0)
+        xs4(0, 0)
+        rg4(0, 1)
         quant("W", 0, 0)
-        il("X", 1, 0, "S")
-        il("D", 1, 0, "V")
+        xs4(1, 0)
+        tr(0, 1)
+        trc2(0, 1)
+        il("W", 2, 0, "S")
         quant("X", 0, 0)
-        xs4(0, 1)
         quant("D", 1, 0)
         quant("X", 1, 0)
-        for m in range(4):
-            dw(0, m, 0)
-        tr(0, 1)
-        il("X", 0, 1, "S")
+        rg(1, 1, 0)
+        rg(1, 1, 1)
+        dw(0, 0, 0)
+        dw(0, 1, 0)
+        xs4(0, 1)
+        rg(1, 1, 2)
+        rg(1, 1, 3)
+        dw(0, 2, 0)
+        dw(0, 3, 0)
+        quant("T", 0, 0)
         xs4(1, 1)
-        il("X", 1, 1, "S")
-        il("W", 1, 0, "V")
-        quant("X", 0, 1)
-        for m in range(4):
-            dw_c(0, m, 0, "S")
         tr(0, 2)
         tr(0, 3)
-        il("W", 2, 0, "V")
-        quant("W", 1, 0)
-        quant("X", 1, 1)
-        trc2(0, 1)
+        for m in range(4):
+            dw_c(0, m, 0, "S")
         trc2(0, 2)
         trc2(0, 3)
+        consts_v()
+        quant("X", 0, 1)
+        quant("W", 1, 0)
+        quant("X", 1, 1)
         for m in range(4):
             dw(0, m, 1)
-        il("W", 3, 0, "V")
-        quant("W", 2, 0)
-        quant("T", 0, 1)
-        il("W", 0, 1, "V")
-        quant("W", 3, 0)
-        quant("T", 0, 2)
+        il("W", 0, 1, "S")
         for m in range(4):
             dw_c(0, m, 1, "S")
             dw_s(0, m)
+        il("W", 3, 0, "V")
+        quant("T", 0, 1)
+        quant("W", 2, 0)
+        quant("T", 0, 2)
+        quant("W", 3, 0)
         quant("T", 0, 3)
-        for j in range(PACK):
-            dx(0, j, 0)
-        il("W", 1, 1, "V")
-        il("W", 2, 1, "S")
-        il("W", 3, 1, "S")
-        quant("W", 0, 1)
+        dx(0, 0, 0)
+        dx(0, 1, 0)
         tr(1, 0)
-        tr(1, 1)
-        ep_a(0, 0, 0)
-        quant("W", 1, 1)
-        ep_a(0, 1, 0)
-        quant("W", 2, 1)
-        ep_a(0, 2, 0)
-        ep_a(0, 3, 0)
-        quant("W", 3, 1)
-        trc2(1, 0)
-        trc2(1, 1)
-        dx(0, 0, 1)
-        il("D", 0, 1, "S")
+        dx(0, 2, 0)
+        dx(0, 3, 0)
+        il("W", 3, 1, "S")
         il("D", 1, 1, "S")
-        quant("T", 1, 0)
-        quant("T", 1, 1)
-        dx(0, 1, 1)
-        tr(1, 2)
-        tr(1, 3)
-        ep_a(0, 0, 1)
+        trc2(1, 0)
+        il("W", 1, 1, "V")
+        quant("W", 0, 1)
+        il("W", 2, 1, "V")
+        quant("W", 1, 1)
         quant("D", 0, 1)
+        quant("W", 2, 1)
+        ep_a(0, 0, 0)
+        quant("W", 3, 1)
+        dx(0, 0, 1)
+        dx(0, 1, 1)
+        ep_a(0, 1, 0)
+        ep_a(0, 2, 0)
+        tr(1, 1)
+        ep_a(0, 3, 0)
+        quant("D", 1, 1)
+        il("D", 0, 2, "S")
+        trc2(1, 1)
+        ep_a(0, 0, 1)
+        quant("T", 1, 0)
+        dw2(1, 0)
         ep_b(0, 0)
         ep_a(0, 1, 1)
+        dw2(1, 1)
+        dx(0, 2, 1)
+        tr(1, 2)
         ep_c(0, 0)
         ep_s(0, 0)
+        out2(1, 0)
+        out2(1, 1)
         trc2(1, 2)
-        trc2(1, 3)
-        dx(0, 2, 1)
-        dx(0, 3, 1)
-        quant("D", 1, 1)
         ep_b(0, 1)
-        quant("T", 1, 2)
+        quant("D", 0, 2)
+        dw2(1, 2)
+        tr(1, 3)
+        dx(0, 3, 1)
+        ep_a(0, 2, 1)
         ep_c(0, 1)
         ep_s(0, 1)
+        out2(1, 2)
+        trc2(1, 3)
+        dw2(1, 3)
+        il("D", 1, 2, "S")
+        ep_b(0, 2)
+        quant("T", 1, 1)
+        quant("T", 1, 2)
         quant("T", 1, 3)
-        dsteps = [("D", g, c) for c in range(2, CHUNKS) for g in range(GROUPS)]
-        dwt = [(c, m) for c in range(1, CHUNKS) for m in range(4)]
-        for s in range(6):
-            g, j = divmod(s + 2, PACK)
-            if s < 4:
-                il(*dsteps[s], "S")
-            for c, m in dwt[2 * s : 2 * s + 2]:
-                dw(c, m, 0)
-                dw(c, m, 1)
-            if g == 1:
-                ep_a(g, j, 0)
-            if s > 0:
-                ep_c(*divmod(s + 1, PACK))
-                ep_s(*divmod(s + 1, PACK))
-            ep_a(g, j, 1)
-            if s < 4:
-                quant(*dsteps[s])
-            ep_b(g, j)
-            for c, m in dwt[2 * s : 2 * s + 2]:
-                dw_c(c, m, 0, "S")
-                dw_c(c, m, 1, "S")
-                dw_s(c, m)
-            if 1 <= s < 5:
-                dx(1, s - 1, 0)
-                dx(1, s - 1, 1)
-        ep_c(1, 3)
-        ep_s(1, 3)
+        dx(1, 0, 0)
+        dx(1, 0, 1)
+        ep_a(0, 3, 1)
+        ep_c(0, 2)
+        ep_s(0, 2)
+        out2(1, 3)
+        quant("D", 1, 2)
+        il("D", 0, 3, "S")
+        dw2(2, 0)
+        dw2(2, 1)
+        ep_b(0, 3)
+        for s in range(PACK):
+            if s < 3:
+                dx(1, s + 1, 0)
+                dx(1, s + 1, 1)
+            ep_a(1, s, 0)
+            ep_a(1, s, 1)
+            ep_c(*divmod(s + 3, PACK))
+            ep_s(*divmod(s + 3, PACK))
+            for c, m in [divmod(8 + 2 * s + k, 4) for k in range(2)]:
+                out2(c, m)
+            if s == 0:
+                il("D", 1, 3, "S")
+            if s < 2:
+                quant("D", s, 3)
+            if s < 3:
+                for c, m in [divmod(10 + 2 * s + k, 4) for k in range(2)]:
+                    dw2(c, m)
+            ep_b(1, s)
+        ep_ch(1, 3, 0)
+        ep_ch(1, 3, 1)

@@ -56,7 +56,7 @@ def tile_attentionlayerdecoder_pa_v_kernel(
         r_col = keep.tile([P, GROUPS * PACK], F32, name="r_col")
         r2_col = keep.tile([P, GROUPS * PACK], F32, name="r2_col")
         coef = keep.tile([P, GROUPS * PACK], F32, name="coef")
-        t_sb = [keep.tile([P, PACK, HD], BF16, name="t%d" % g) for g in range(GROUPS)]
+        t_sb = [keep.tile([P, HALVES, PACK, HALF], BF16, name="t%d" % g) for g in range(GROUPS)]
         codes = {}
         scales = {}
         free_banks = list(range(BANKS))
@@ -92,6 +92,9 @@ def tile_attentionlayerdecoder_pa_v_kernel(
         def cols(h):
             return slice(h * HALF, (h + 1) * HALF)
 
+        def by_half(tile):
+            return tile[:].rearrange("p (h c) -> p h c", h=HALVES)
+
         def copy_on(engine, out, in_):
             if engine == "V":
                 nc.vector.tensor_copy(out=out, in_=in_)
@@ -107,7 +110,7 @@ def tile_attentionlayerdecoder_pa_v_kernel(
 
         def load_t(g, h):
             rows = tokens[0, g * K_PASS : (g + 1) * K_PASS, cols(h)]
-            nc.sync.dma_start(out=t_sb[g][:, :, cols(h)], in_=rows.rearrange("(p j) c -> p j c", j=PACK))
+            nc.sync.dma_start(out=t_sb[g][:, h, :, :], in_=rows.rearrange("(p j) c -> p j c", j=PACK))
 
         def load_w(c, h):
             tile = new_slot(("raw", "W", c, h), [P, PACK, HALF], BF16, 1)
@@ -165,13 +168,12 @@ def tile_attentionlayerdecoder_pa_v_kernel(
         def xs(g, h, q):
             if q == 0:
                 new_packed(("X", g, h))
-            first = h * HALF + q * P
             nc.vector.tensor_tensor(
                 out=slot_of["packed", "X", g, h][1][:, q * HALF : (q + 1) * HALF].rearrange(
-                    "p (c i j) -> p c j i", i=4, j=PACK
+                    "p (c i j) -> p c j i", i=2, j=PACK
                 ),
-                in0=last_read(("rg", g, h, q))[:].rearrange("p j (c i) -> p c j i", i=4),
-                in1=t_sb[g][:, :, first : first + P].rearrange("p j (c i) -> p c j i", i=4),
+                in0=last_read(("rg", g, h, q))[:].rearrange("p j (c i) -> p c j i", i=2),
+                in1=t_sb[g][:, h, :, q * P : (q + 1) * P].rearrange("p j (c i) -> p c j i", i=2),
                 op=MULT,
             )
 
@@ -282,22 +284,22 @@ def tile_attentionlayerdecoder_pa_v_kernel(
             tile = new_slot(("res", g, j), [P, HD], F32, 1)
             col = g * PACK + j
             nc.vector.scalar_tensor_tensor(
-                out=tile[:], in0=use(("dhr", g, j))[:], scalar=r2_col[:, col : col + 1], in1=t_sb[g][:, j, :],
+                out=by_half(tile), in0=by_half(use(("dhr", g, j))), scalar=r2_col[:, col : col + 1], in1=t_sb[g][:, :, j, :],
                 op0=MULT, op1=MULT, accum_out=coef[:, col : col + 1],
             )
 
         def ep_c(g, j):
             col = g * PACK + j
             nc.vector.scalar_tensor_tensor(
-                out=slot_of["res", g, j][1][:], in0=t_sb[g][:, j, :], scalar=coef[:, col : col + 1],
-                in1=use(("dhr", g, j))[:], op0=MULT, op1=ADD,
+                out=by_half(slot_of["res", g, j][1]), in0=t_sb[g][:, :, j, :], scalar=coef[:, col : col + 1],
+                in1=by_half(use(("dhr", g, j))), op0=MULT, op1=ADD,
             )
 
         def ep_ch(g, j, h):
             col = g * PACK + j
             res = slot_of["res", g, j][1]
             nc.vector.scalar_tensor_tensor(
-                out=res[:, cols(h)], in0=t_sb[g][:, j, cols(h)], scalar=coef[:, col : col + 1],
+                out=res[:, cols(h)], in0=t_sb[g][:, h, j, :], scalar=coef[:, col : col + 1],
                 in1=slot_of["dhr", g, j][1][:, cols(h)], op0=MULT, op1=ADD,
             )
             rows = out_0[0, g * K_PASS : (g + 1) * K_PASS, cols(h)].rearrange("(p j) c -> p j c", j=PACK)

from contextlib import ExitStack

import concourse.mybir as mybir
from concourse.masks import make_identity

F32 = mybir.dt.float32
BF16 = mybir.dt.bfloat16
U32 = mybir.dt.uint32
U8 = mybir.dt.uint8
E4M3X4 = mybir.dt.float8_e4m3fn_x4
E5M2X4 = mybir.dt.float8_e5m2_x4
MULT = mybir.AluOpType.mult
ADD = mybir.AluOpType.add
SUB = mybir.AluOpType.subtract

P = 128
PACK = 4
K_PASS = P * PACK
HALF = 512
N_TOK = 1024
HD = 1024
HEAD_DIM = 128
GROUPS = N_TOK // K_PASS
CHUNKS = 4
HALVES = HD // HALF
BANKS = 8
FLOPS = 2 * 2 * N_TOK * HD * CHUNKS * K_PASS

SLOTS = 34


def tile_attentionlayerdecoder_pa_v_kernel(
    tc, tokens, norm_w, Wq, bq, Wk, bk, Wv, bv, rstd, grad_0, grad_1, grad_2, out_0, out_1, out_2, out_3
):
    nc = tc.nc
    grad_of = [(grad_0, 0), (grad_0, 4), (grad_1, 0), (grad_2, 0)]
    w_of = [Wq[0:K_PASS, :], Wq[K_PASS : 2 * K_PASS, :], Wk, Wv]
    dw_of = [out_1[0:K_PASS, :], out_1[K_PASS : 2 * K_PASS, :], out_2, out_3]

    with ExitStack() as ctx:
        keep = ctx.enter_context(tc.tile_pool(name="keep", bufs=1))
        stage = ctx.enter_context(tc.tile_pool(name="stage", bufs=1))
        psum = ctx.enter_context(tc.psum_pool(name="psum", bufs=1))
        ctx.enter_context(tc.manual_schedule())

        ident_bf = keep.tile([P, P], BF16, name="ident_bf")
        make_identity(nc, ident_bf[:])
        gain = keep.tile([P, HD], BF16, name="gain")
        r_parts = keep.tile([P, GROUPS * PACK, P], BF16, name="r_parts")
        r_rows = keep.tile([P, GROUPS * PACK, P], BF16, name="r_rows")
        r_rest = keep.tile([P, GROUPS * PACK], F32, name="r_rest")
        nc.gpsimd.memset(r_parts[:].rearrange("p a b -> p (a b)").bitcast(F32), 0.0)
        ident = keep.tile([P, P], F32, name="ident")
        make_identity(nc, ident[:])
        gain_cols_bf = keep.tile([P, HALVES, PACK], BF16, name="gain_cols_bf")
        r_col = keep.tile([P, GROUPS * PACK], F32, name="r_col")
        r2_col = keep.tile([P, GROUPS * PACK], F32, name="r2_col")
        coef = keep.tile([P, GROUPS * PACK], F32, name="coef")
        t_sb = [keep.tile([P, HALVES, PACK, HALF], BF16, name="t%d" % g) for g in range(GROUPS)]
        codes = {}
        scales = {}
        free_banks = list(range(BANKS))
        bank_of = {}

        def new_bank(key, shape, dtype):
            number = free_banks.pop(0)
            bank = psum.tile(shape, dtype, name="bank", tag="bank%d" % number)
            bank_of[key] = (number, bank)
            return bank

        def last_read(key):
            number, bank = bank_of.pop(key)
            free_banks.append(number)
            return bank

        free_slots = list(range(SLOTS))
        slot_of = {}

        def new_slot(key, shape, dtype, uses):
            number = free_slots.pop(0)
            tile = stage.tile(shape, dtype, name="slot", tag="slot%d" % number, align_bytes=64)
            slot_of[key] = [number, tile, uses]
            return tile

        def use(key):
            entry = slot_of[key]
            entry[2] = entry[2] - 1
            if entry[2] == 0:
                free_slots.append(entry[0])
            return entry[1]

        def cols(h):
            return slice(h * HALF, (h + 1) * HALF)

        def by_half(tile):
            return tile[:].rearrange("p (h c) -> p h c", h=HALVES)

        def copy_on(engine, out, in_):
            if engine == "V":
                nc.vector.tensor_copy(out=out, in_=in_)
            else:
                nc.scalar.copy(out=out, in_=in_)

        def load_small():
            nc.sync.dma_start(out=gain_cols_bf[:], in_=norm_w.rearrange("(h p i) -> p h i", h=HALVES, i=PACK))
            nc.sync.dma_start(
                out=r_col[:].rearrange("p (g j) -> p g j", g=GROUPS),
                in_=rstd[0].rearrange("(g p j) o -> p g (j o)", g=GROUPS, j=PACK),
            )

        def load_t(g, h):
            rows = tokens[0, g * K_PASS : (g + 1) * K_PASS, cols(h)]
            nc.sync.dma_start(out=t_sb[g][:, h, :, :], in_=rows.rearrange("(p j) c -> p j c", j=PACK))

        def load_w(c, h):
            tile = new_slot(("raw", "W", c, h), [P, PACK, HALF], BF16, 1)
            nc.sync.dma_start(out=tile[:], in_=w_of[c][:, cols(h)].rearrange("(p j) n -> p j n", j=PACK))

        def load_dy(g, c):
            tile = new_slot(("raw", "D", g, c), [P, PACK, K_PASS], BF16, 2)
            grad, first = grad_of[c]
            for hh in range(K_PASS // HEAD_DIM):
                rows = grad[0, first + hh, g * K_PASS : (g + 1) * K_PASS, :]
                nc.sync.dma_start(
                    out=tile[:, :, hh * HEAD_DIM : (hh + 1) * HEAD_DIM],
                    in_=rows.rearrange("(p j) d -> p j d", j=PACK),
                )

        def consts_v():
            nc.vector.scalar_tensor_tensor(
                out=r2_col[:], in0=r_col[:], scalar=-1.0 / HD, in1=r_col[:], op0=MULT, op1=MULT
            )

        def gain_t(h):
            bank = new_bank(("gain", h), [P, PACK, P], BF16)
            for i in range(PACK):
                nc.tensor.transpose(bank[:, i, :], gain_cols_bf[:, h, i : i + 1].to_broadcast([P, P]), ident_bf[:])

        def gain_c(h, engine):
            copy_on(
                engine,
                gain[:, cols(h)].rearrange("p (n i) -> p n i", i=PACK),
                last_read(("gain", h))[:].rearrange("p i n -> p n i"),
            )

        def r_split():
            nc.vector.tensor_copy(out=r_parts[:, :, 0], in_=r_col[:])
            nc.vector.tensor_tensor(out=r_rest[:], in0=r_col[:], in1=r_parts[:, :, 0], op=SUB)
            nc.vector.tensor_copy(out=r_parts[:, :, 1], in_=r_rest[:])
            nc.vector.tensor_tensor(out=r_parts[:, :, 2], in0=r_rest[:], in1=r_parts[:, :, 1], op=SUB)

        def r_t():
            bank = new_bank("r", [P, GROUPS * PACK, P], BF16)
            for col in range(GROUPS * PACK):
                nc.tensor.transpose(bank[:, col, :], r_parts[:, col, :], ident_bf[:])

        def r_c():
            nc.scalar.copy(out=r_rows[:], in_=last_read("r")[:])

        def rg(g, h, q):
            bank = new_bank(("rg", g, h, q), [P, PACK, P], F32)
            first = h * HALF + q * P
            for j in range(PACK):
                nc.tensor.matmul(
                    bank[:, j, :], lhsT=r_rows[:, g * PACK + j, :], rhs=gain[:, first : first + P], start=True, stop=True
                )

        def xs(g, h, q):
            if q == 0:
                new_packed(("X", g, h))
            nc.vector.tensor_tensor(
                out=slot_of["packed", "X", g, h][1][:, q * HALF : (q + 1) * HALF].rearrange(
                    "p (c i j) -> p c j i", i=2, j=PACK
                ),
                in0=last_read(("rg", g, h, q))[:].rearrange("p j (c i) -> p c j i", i=2),
                in1=t_sb[g][:, h, :, q * P : (q + 1) * P].rearrange("p j (c i) -> p c j i", i=2),
                op=MULT,
            )

        def new_packed(key):
            return new_slot(("packed",) + key, [P, PACK * HALF], BF16, 1)

        def il(kind, a, b, engine):
            tile = new_packed((kind, a, b))
            copy_on(
                engine,
                tile[:].rearrange("p (c i t) -> p c t i", i=4, t=PACK),
                use(("raw", kind, a, b))[:].rearrange("p t (c i) -> p c t i", i=4),
            )

        def il_pe(kind, a, b):
            source = use(("raw", kind, a, b))
            for half in range(2):
                bank = new_bank(("il", kind, a, b, half), [P, 2, HALF], BF16)
                for q in range(2):
                    first = (2 * half + q) * P
                    nc.tensor.matmul(
                        bank[:, q, :].rearrange("p (c t) -> p c t", t=PACK),
                        lhsT=ident_bf[:],
                        rhs=source[:, :, first : first + P].rearrange("p t c -> p c t"),
                        start=True,
                        stop=True,
                    )

        def il_c(kind, a, b, half, engine):
            if half == 0:
                new_packed((kind, a, b))
            copy_on(
                engine,
                slot_of["packed", kind, a, b][1][:, half * 2 * HALF : (half + 1) * 2 * HALF],
                last_read(("il", kind, a, b, half))[:].rearrange("p q n -> p (q n)"),
            )

        def quant(kind, a, b):
            name = "%s%d%d" % (kind, a, b)
            code_tile = keep.tile([P, HALF], U32, name="codes" + name, align_bytes=64)
            scale_tile = keep.tile([P, HALF], U8, name="scales" + name, align_bytes=64)
            codes[kind, a, b] = code_tile
            scales[kind, a, b] = scale_tile
            fmt = E5M2X4 if kind in ("D", "T") else E4M3X4
            nc.vector.quantize_mx(out=code_tile[:].bitcast(fmt), scales=scale_tile[:], in_=use(("packed", kind, a, b))[:])

        def tr(g, c):
            words = use(("raw", "D", g, c))[:].rearrange("p j f -> p (j f)").bitcast(F32)
            for b in range(2):
                bank = new_bank(("T", g, c, b), [P, 2, 2, P], F32)
                for jj in range(2):
                    first = (2 * b + jj) * 2 * P
                    for u in range(2):
                        nc.tensor.transpose(bank[:, jj, u, :], words[:, first + u : first + 2 * P : 2], ident[:])

        def tr_c(g, c, b, engine):
            if b == 0:
                new_packed(("T", g, c))
            words = slot_of["packed", "T", g, c][1][:].bitcast(F32)
            copy_on(
                engine,
                words[:, b * HALF : (b + 1) * HALF].rearrange("q (jj p u) -> q jj p u", jj=2, u=2),
                last_read(("T", g, c, b))[:].rearrange("q jj u p -> q jj p u"),
            )

        def mx_group(bank, left, first, right):
            for n in range(len(left)):
                nc.tensor.matmul_mx(
                    out=bank[:],
                    lhsT=codes[left[n]][:, first : first + P].bitcast(E5M2X4),
                    lhsT_scale=scales[left[n]][:, first : first + P],
                    rhs=codes[right[n]][:].bitcast(E4M3X4),
                    rhs_scale=scales[right[n]][:],
                    start=(n == 0),
                    stop=(n == len(left) - 1),
                )

        def dx(g, j, h):
            bank = new_bank(("dx", g, j, h), [P, HALF], F32)
            mx_group(bank, [("T", g, c) for c in range(CHUNKS)], j * P, [("W", c, h) for c in range(CHUNKS)])

        def dw(c, m, h):
            bank = new_bank(("dw", c, m, h), [P, HALF], F32)
            mx_group(bank, [("D", g, c) for g in range(GROUPS)], m * P, [("X", g, h) for g in range(GROUPS)])

        def dw_c(c, m, h, engine):
            if ("dwo", c, m) not in slot_of:
                new_slot(("dwo", c, m), [P, HD], F32, 2)
            copy_on(engine, slot_of["dwo", c, m][1][:, cols(h)], last_read(("dw", c, m, h))[:])

        def dw_s(c, m):
            use(("dwo", c, m))
            nc.sync.dma_start(out=dw_of[c][m * P : (m + 1) * P, :], in_=use(("dwo", c, m))[:])

        def dw_sh(c, m, h):
            nc.sync.dma_start(out=dw_of[c][m * P : (m + 1) * P, cols(h)], in_=use(("dwo", c, m))[:, cols(h)])

        def ep_a(g, j, h):
            if h == 0:
                new_slot(("dhr", g, j), [P, HD], F32, 2)
            col = g * PACK + j
            nc.vector.scalar_tensor_tensor(
                out=slot_of["dhr", g, j][1][:, cols(h)], in0=last_read(("dx", g, j, h))[:], scalar=r_col[:, col : col + 1],
                in1=gain[:, cols(h)], op0=MULT, op1=MULT,
            )

        def ep_b(g, j):
            tile = new_slot(("res", g, j), [P, HD], F32, 1)
            col = g * PACK + j
            nc.vector.scalar_tensor_tensor(
                out=by_half(tile), in0=by_half(use(("dhr", g, j))), scalar=r2_col[:, col : col + 1], in1=t_sb[g][:, :, j, :],
                op0=MULT, op1=MULT, accum_out=coef[:, col : col + 1],
            )

        def ep_c(g, j):
            col = g * PACK + j
            nc.vector.scalar_tensor_tensor(
                out=by_half(slot_of["res", g, j][1]), in0=t_sb[g][:, :, j, :], scalar=coef[:, col : col + 1],
                in1=by_half(use(("dhr", g, j))), op0=MULT, op1=ADD,
            )

        def ep_ch(g, j, h):
            col = g * PACK + j
            res = slot_of["res", g, j][1]
            nc.vector.scalar_tensor_tensor(
                out=res[:, cols(h)], in0=t_sb[g][:, h, j, :], scalar=coef[:, col : col + 1],
                in1=slot_of["dhr", g, j][1][:, cols(h)], op0=MULT, op1=ADD,
            )
            rows = out_0[0, g * K_PASS : (g + 1) * K_PASS, cols(h)].rearrange("(p j) c -> p j c", j=PACK)
            nc.sync.dma_start(out=rows[:, j, :], in_=res[:, cols(h)])

        def ep_s(g, j):
            rows = out_0[0, g * K_PASS : (g + 1) * K_PASS, :].rearrange("(p j) c -> p j c", j=PACK)
            nc.sync.dma_start(out=rows[:, j, :], in_=use(("res", g, j))[:])

        load_small()
        load_dy(0, 0)
        load_w(0, 0)
        load_t(0, 0)
        load_dy(1, 0)
        load_t(1, 0)
        load_w(1, 0)
        load_t(0, 1)
        load_dy(0, 1)
        load_t(1, 1)
        load_w(2, 0)
        load_dy(0, 2)
        load_w(3, 0)
        load_dy(0, 3)
        for c in range(CHUNKS):
            load_w(c, 1)
        for c in range(1, CHUNKS):
            load_dy(1, c)

        def rg4(g, h):
            for q in range(PACK):
                rg(g, h, q)

        def xs4(g, h):
            for q in range(PACK):
                xs(g, h, q)

        def trc2(g, c):
            tr_c(g, c, 0, "S")
            tr_c(g, c, 1, "S")

        def dw2(c, m):
            dw(c, m, 0)
            dw(c, m, 1)

        def out2(c, m):
            dw_c(c, m, 0, "S")
            dw_c(c, m, 1, "S")
            dw_s(c, m)


        r_split()
        gain_t(0)
        gain_t(1)
        r_t()
        gain_c(0, "S")
        r_c()
        gain_c(1, "S")
        il("D", 0, 0, "V")
        il("W", 0, 0, "V")
        tr(0, 0)
        rg4(0, 0)
        trc2(0, 0)
        rg4(1, 0)
        il("D", 1, 0, "S")
        il("W", 1, 0, "S")
        il("D", 0, 1, "S")
        quant("D", 0, 0)
        xs4(0, 0)
        rg4(0, 1)
        quant("W", 0, 0)
        xs4(1, 0)
        tr(0, 1)
        trc2(0, 1)
        il("W", 2, 0, "S")
        quant("X", 0, 0)
        quant("D", 1, 0)
        quant("X", 1, 0)
        rg(1, 1, 0)
        rg(1, 1, 1)
        dw(0, 0, 0)
        dw(0, 1, 0)
        xs4(0, 1)
        rg(1, 1, 2)
        rg(1, 1, 3)
        dw(0, 2, 0)
        dw(0, 3, 0)
        quant("T", 0, 0)
        xs4(1, 1)
        tr(0, 2)
        tr(0, 3)
        for m in range(4):
            dw_c(0, m, 0, "S")
        trc2(0, 2)
        trc2(0, 3)
        consts_v()
        quant("X", 0, 1)
        quant("W", 1, 0)
        quant("X", 1, 1)
        for m in range(4):
            dw(0, m, 1)
        il("W", 0, 1, "S")
        for m in range(4):
            dw_c(0, m, 1, "S")
            dw_s(0, m)
        il("W", 3, 0, "V")
        quant("T", 0, 1)
        quant("W", 2, 0)
        quant("T", 0, 2)
        quant("W", 3, 0)
        quant("T", 0, 3)
        dx(0, 0, 0)
        dx(0, 1, 0)
        tr(1, 0)
        dx(0, 2, 0)
        dx(0, 3, 0)
        il("W", 3, 1, "S")
        il("D", 1, 1, "S")
        trc2(1, 0)
        il("W", 1, 1, "V")
        quant("W", 0, 1)
        il("W", 2, 1, "V")
        quant("W", 1, 1)
        quant("D", 0, 1)
        quant("W", 2, 1)
        ep_a(0, 0, 0)
        quant("W", 3, 1)
        dx(0, 0, 1)
        dx(0, 1, 1)
        ep_a(0, 1, 0)
        ep_a(0, 2, 0)
        tr(1, 1)
        ep_a(0, 3, 0)
        quant("D", 1, 1)
        il("D", 0, 2, "S")
        trc2(1, 1)
        ep_a(0, 0, 1)
        quant("T", 1, 0)
        dw2(1, 0)
        ep_b(0, 0)
        ep_a(0, 1, 1)
        dw2(1, 1)
        dx(0, 2, 1)
        tr(1, 2)
        ep_c(0, 0)
        ep_s(0, 0)
        out2(1, 0)
        out2(1, 1)
        trc2(1, 2)
        ep_b(0, 1)
        quant("D", 0, 2)
        dw2(1, 2)
        tr(1, 3)
        dx(0, 3, 1)
        ep_a(0, 2, 1)
        ep_c(0, 1)
        ep_s(0, 1)
        out2(1, 2)
        trc2(1, 3)
        dw2(1, 3)
        il("D", 1, 2, "S")
        ep_b(0, 2)
        quant("T", 1, 1)
        quant("T", 1, 2)
        quant("T", 1, 3)
        dx(1, 0, 0)
        dx(1, 0, 1)
        ep_a(0, 3, 1)
        ep_c(0, 2)
        ep_s(0, 2)
        out2(1, 3)
        quant("D", 1, 2)
        il("D", 0, 3, "S")
        dw2(2, 0)
        dw2(2, 1)
        ep_b(0, 3)
        for s in range(PACK):
            if s < 3:
                dx(1, s + 1, 0)
                dx(1, s + 1, 1)
            ep_a(1, s, 0)
            ep_a(1, s, 1)
            ep_c(*divmod(s + 3, PACK))
            ep_s(*divmod(s + 3, PACK))
            for c, m in [divmod(8 + 2 * s + k, 4) for k in range(2)]:
                out2(c, m)
            if s == 0:
                il("D", 1, 3, "S")
            if s < 2:
                quant("D", s, 3)
            if s < 3:
                for c, m in [divmod(10 + 2 * s + k, 4) for k in range(2)]:
                    dw2(c, m)
            ep_b(1, s)
        ep_ch(1, 3, 0)
        ep_ch(1, 3, 1)
